import numpy as np
import ml_dtypes


def mxq(x, axis, fmt="e4m3"):
    dtype, down = {"e4m3": (ml_dtypes.float8_e4m3fn, 7), "e5m2": (ml_dtypes.float8_e5m2, 14)}[fmt]
    v = np.moveaxis(np.asarray(x, np.float32).astype(ml_dtypes.bfloat16).astype(np.float64), axis, -1)
    blocks = v.reshape(v.shape[:-1] + (-1, 32))
    amax = np.abs(blocks).max(-1, keepdims=True)
    byte = np.maximum(np.where(amax > 0, np.frexp(amax)[1] - 1 + 127, 0) - down, 1)
    scale = np.exp2(byte - 127.0)
    codes = (blocks / scale).astype(np.float32).astype(dtype).astype(np.float64)
    return np.moveaxis((codes * scale).reshape(v.shape), -1, axis)


WIDE = False


def mx_kscale(k):
    if not WIDE:
        return np.ones(k)
    levels = np.array([10, -10, 5, -5, 0])
    if k % 512:
        return np.exp2(np.random.permutation(np.resize(levels, k // 32))).repeat(32)
    a = np.empty((k // 512, 16))
    for p in range(k // 512):
        a[p, :8] = np.random.permutation(np.resize(levels, 8))
        for g in range(8):
            far = levels[np.abs(levels - a[p, g]) >= 10]
            a[p, g + 8] = far[np.random.randint(len(far))]
    return np.exp2(a.ravel()).repeat(32)


BF16 = ml_dtypes.bfloat16


def bf(x):
    return np.asarray(x, np.float32).astype(BF16)


def f64(x):
    return np.asarray(x).astype(np.float64)


B, NH, T, D, N, CK = 1, 2, 8192, 256, 256, 512
KD = NH * N
EPS_LN = 1e-5
TARGET_ACTIVITY = 0.1


def layernorm(v):
    m = np.mean(v, axis=-1, keepdims=True)
    var = np.mean((v - m) ** 2, axis=-1, keepdims=True)
    return (v - m) / np.sqrt(var + EPS_LN)


def setup_inputs():
    t = mx_kscale(KD)
    xy = np.maximum(np.random.standard_normal((B, NH, T, N)) * 0.5, 0.0) * np.maximum(np.random.standard_normal((B, NH, T, N)), 0.0)
    return {'xy_sparse': bf(xy * t.reshape(NH, 1, N)),
            'decoder': bf(np.random.standard_normal((KD, D)) * 2.0 / np.sqrt(KD) / t[:, None]),
            'x': bf(np.random.standard_normal((B, 1, T, D))),
            'scale': bf(1.0 + 0.1 * np.random.standard_normal(D)),
            'running_activity': bf(TARGET_ACTIVITY * np.exp(0.5 * np.random.standard_normal(D)))}


def reference(xy_sparse, decoder, x, scale, running_activity):
    flat = f64(xy_sparse).transpose(0, 2, 1, 3).reshape(B, 1, T, KD)
    y_mlp = mxq(flat, 3, 'e4m3') @ mxq(f64(decoder), 0, 'e4m3')
    y = layernorm(y_mlp)
    regulation = TARGET_ACTIVITY / (f64(running_activity) + 1e-6)
    y = y * np.sqrt(regulation) * f64(scale)
    return layernorm(f64(x) + y)

@@ -1,0 +1,299 @@
+from contextlib import ExitStack
+
+import concourse.masks as masks
+import concourse.mybir as mybir
+
+F32 = mybir.dt.float32
+BF16 = mybir.dt.bfloat16
+U32 = mybir.dt.uint32
+U8 = mybir.dt.uint8
+FP8X4 = mybir.dt.float8_e4m3fn_x4
+ALU = mybir.AluOpType
+ACT = mybir.ActivationFunctionType
+
+P = 128
+HEADS = 2
+HEAD_DIM = 256
+K = HEADS * HEAD_DIM
+PACK = 4
+WORDS = K // 2
+PAIRS = PACK // 2
+D = 256
+T = 8192
+TILES = 4
+BANK_TILES = 2
+BANKS = TILES // BANK_TILES
+GROUPS = T // (P * TILES)
+EPS_LN = 1e-5
+EPS_ACTIVITY = 1e-6
+TARGET_ACTIVITY = 0.1
+
+FLOPS = 2 * T * K * D
+
+
+def tile_bdhlayer_pc_t_kernel(tc, xy_sparse, decoder, x, scale, running_activity, out):
+    nc = tc.nc
+
+    xy_groups = xy_sparse[0].rearrange("h (g p j) n -> g h p j n", p=P, j=TILES)
+    x_groups = x.flatten_outer_dims().rearrange("(g p j) d -> g p (j d)", p=P, j=TILES)
+    out_groups = out.flatten_outer_dims().rearrange("(g p j) d -> g p j d", p=P, j=TILES)
+
+    with ExitStack() as ctx:
+        const = ctx.enter_context(tc.tile_pool(name="const", bufs=1))
+        inputs = ctx.enter_context(tc.tile_pool(name="inputs", bufs=GROUPS))
+        quant = ctx.enter_context(tc.tile_pool(name="quant", bufs=2))
+        work = ctx.enter_context(tc.tile_pool(name="work", bufs=3))
+        results = ctx.enter_context(tc.tile_pool(name="results", bufs=4))
+        stats = ctx.enter_context(tc.tile_pool(name="stats", bufs=3))
+        turned_pool = ctx.enter_context(tc.psum_pool(name="turned", bufs=2 * BANKS))
+        product_pool = ctx.enter_context(tc.psum_pool(name="product", bufs=2 * BANKS))
+
+        xy_tiles = []
+        x_tiles = []
+        rows = const.tile([P, 2, D], BF16)
+        dec_raw = const.tile([P, PACK, D], BF16)
+        nc.vector.memset(rows[:], 0.0)
+        for g in range(GROUPS):
+            xy_sb = inputs.tile([P, TILES, HEADS, HEAD_DIM], BF16)
+            for h in range(HEADS):
+                nc.sync.dma_start(out=xy_sb[:, :, h, :], in_=xy_groups[g, h])
+            xy_tiles.append(xy_sb)
+            if g == 0:
+                nc.sync.dma_start(out=rows[0:1, 0, :], in_=scale.rearrange("(o d) -> o d", o=1))
+                nc.sync.dma_start(out=rows[0:1, 1, :], in_=running_activity.rearrange("(o d) -> o d", o=1))
+                nc.sync.dma_start(
+                    out=dec_raw[:].rearrange("p t d -> p (t d)"),
+                    in_=decoder.rearrange("(p t) d -> p (t d)", t=PACK),
+                )
+            x_sb = inputs.tile([P, TILES, D], BF16)
+            nc.sync.dma_start(out=x_sb[:].rearrange("p j d -> p (j d)"), in_=x_groups[g])
+            x_tiles.append(x_sb)
+
+        ident = const.tile([P, P], F32)
+        masks.make_identity(nc, ident[:])
+        ones = const.tile([P, P], BF16)
+        nc.vector.memset(ones[:], 1.0)
+        eps_ln = const.tile([P, 1], F32)
+        nc.vector.memset(eps_ln[:], EPS_LN)
+        eps_activity = const.tile([P, 1], F32)
+        nc.vector.memset(eps_activity[:], EPS_ACTIVITY / TARGET_ACTIVITY)
+        dec_codes = const.tile([P, D], U32, align_bytes=64)
+        dec_scales = const.tile([P, D], U8, align_bytes=64)
+        gain = const.tile([P, D], F32)
+
+        def quantise_decoder():
+            dec_grouped = const.tile([P, D, PACK], BF16, align_bytes=64)
+            nc.vector.tensor_copy(out=dec_grouped[:], in_=dec_raw[:].rearrange("p t d -> p d t"))
+            nc.vector.quantize_mx(
+                out=dec_codes[:].bitcast(FP8X4),
+                scales=dec_scales[:],
+                in_=dec_grouped[:].rearrange("p d t -> p (d t)"),
+            )
+
+        def make_gain():
+            spread = product_pool.tile([P, BANK_TILES, D], F32, tag="product")
+            nc.tensor.matmul(
+                spread[:].rearrange("p a d -> p (a d)"),
+                lhsT=ones[:],
+                rhs=rows[:].rearrange("p a d -> p (a d)"),
+                start=True,
+                stop=True,
+            )
+            regulation = const.tile([P, D], F32)
+            nc.scalar.activation(
+                out=regulation[:],
+                in_=spread[:, 1, :],
+                func=ACT.Abs_reciprocal_sqrt,
+                scale=1.0 / TARGET_ACTIVITY,
+                bias=eps_activity[:, 0:1],
+            )
+            nc.vector.tensor_tensor(out=gain[:], in0=regulation[:], in1=spread[:, 0, :], op=ALU.mult)
+
+        turned_of = {}
+        grouped_of = {}
+        codes_of = {}
+        scales_of = {}
+        products_of = {}
+        moments_of = {}
+        rstd_of = {}
+        centred_of = {}
+        z_of = {}
+        z_sum_of = {}
+        square_sum_of = {}
+        rstd2_of = {}
+        shift_of = {}
+
+        def turn(g):
+            xy_words = xy_tiles[g][:].rearrange("p j h n -> p (j h n)").bitcast(F32)
+            turned_of[g] = []
+            for b in range(BANKS):
+                turned = turned_pool.tile([P, BANK_TILES, PAIRS, P], F32)
+                turned_of[g].append(turned)
+                for a in range(BANK_TILES):
+                    first = (BANK_TILES * b + a) * WORDS
+                    for u in range(PAIRS):
+                        words = slice(first + u, first + WORDS, PAIRS)
+                        nc.tensor.transpose(turned[:, a, u, :], xy_words[:, words], ident[:])
+
+        def regroup(g, b):
+            if b == 0:
+                grouped = quant.tile([P, BANKS, BANK_TILES * K], BF16, align_bytes=64)
+                grouped_of[g] = grouped
+            nc.scalar.copy(
+                out=grouped_of[g][:, b, :].bitcast(F32).rearrange("p (a t u) -> p a t u", a=BANK_TILES, u=PAIRS),
+                in_=turned_of[g][b][:].rearrange("p a u t -> p a t u"),
+            )
+
+        def quantise(g):
+            codes = quant.tile([P, BANKS, BANK_TILES * P], U32, align_bytes=64)
+            scales = quant.tile([P, BANKS, BANK_TILES * P], U8, align_bytes=64)
+            codes_of[g] = codes
+            scales_of[g] = scales
+            for b in range(BANKS):
+                nc.vector.quantize_mx(
+                    out=codes[:, b, :].bitcast(FP8X4), scales=scales[:, b, :], in_=grouped_of[g][:, b, :]
+                )
+
+        def multiply(g):
+            products_of[g] = []
+            for b in range(BANKS):
+                product = product_pool.tile([P, BANK_TILES, D], F32)
+                products_of[g].append(product)
+                for a in range(BANK_TILES):
+                    tokens = slice(P * a, P * (a + 1))
+                    nc.tensor.matmul_mx(
+                        out=product[:, a, :],
+                        lhsT=codes_of[g][:, b, tokens].bitcast(FP8X4),
+                        lhsT_scale=scales_of[g][:, b, tokens],
+                        rhs=dec_codes[:].bitcast(FP8X4),
+                        rhs_scale=dec_scales[:],
+                        start=True,
+                        stop=True,
+                    )
+
+        def first_moments(g):
+            moments = stats.tile([P, TILES, 3], F32)
+            moments_of[g] = moments
+            for b in range(BANKS):
+                nc.vector.bn_stats(
+                    out=moments[:, BANK_TILES * b : BANK_TILES * (b + 1), :].rearrange("p a m -> p (a m)"),
+                    in_=products_of[g][b][:].rearrange("p a d -> p d a"),
+                )
+
+        def first_root(g):
+            rstd = stats.tile([P, TILES], F32)
+            rstd_of[g] = rstd
+            nc.scalar.activation(
+                out=rstd[:],
+                in_=moments_of[g][:, :, 2],
+                func=ACT.Abs_reciprocal_sqrt,
+                scale=1.0 / float(D),
+                bias=eps_ln[:, 0:1],
+            )
+
+        def centre(g):
+            centred = work.tile([P, TILES, D], F32)
+            centred_of[g] = centred
+            for j in range(TILES):
+                nc.vector.scalar_tensor_tensor(
+                    out=centred[:, j, :],
+                    in0=products_of[g][j // BANK_TILES][:, j % BANK_TILES, :],
+                    scalar=moments_of[g][:, j, 1:2],
+                    in1=gain[:],
+                    op0=ALU.subtract,
+                    op1=ALU.mult,
+                )
+
+        def residual(g):
+            z = work.tile([P, TILES, D], F32)
+            z_sum = stats.tile([P, TILES], F32)
+            z_of[g] = z
+            z_sum_of[g] = z_sum
+            for j in range(TILES):
+                nc.vector.scalar_tensor_tensor(
+                    out=z[:, j, :],
+                    in0=centred_of[g][:, j, :],
+                    scalar=rstd_of[g][:, j : j + 1],
+                    in1=x_tiles[g][:, j, :],
+                    op0=ALU.mult,
+                    op1=ALU.add,
+                    accum_out=z_sum[:, j : j + 1],
+                )
+
+        def second_squares(g):
+            squares = work.tile([P, TILES, D], BF16)
+            square_sum = stats.tile([P, TILES], F32)
+            square_sum_of[g] = square_sum
+            for j in range(TILES):
+                nc.scalar.activation(
+                    out=squares[:, j, :],
+                    in_=z_of[g][:, j, :],
+                    func=ACT.Square,
+                    scale=-float(D),
+                    bias=z_sum_of[g][:, j : j + 1],
+                    accum_out=square_sum[:, j : j + 1],
+                )
+
+        def second_root(g):
+            rstd2 = stats.tile([P, TILES], F32)
+            rstd2_of[g] = rstd2
+            nc.scalar.activation(
+                out=rstd2[:],
+                in_=square_sum_of[g][:],
+                func=ACT.Abs_reciprocal_sqrt,
+                scale=1.0 / float(D * D * D),
+                bias=eps_ln[:, 0:1],
+            )
+
+        def second_shift(g):
+            shift = stats.tile([P, TILES], F32)
+            shift_of[g] = shift
+            nc.vector.scalar_tensor_tensor(
+                out=shift[:],
+                in0=z_sum_of[g][:],
+                scalar=-1.0 / float(D),
+                in1=rstd2_of[g][:],
+                op0=ALU.mult,
+                op1=ALU.mult,
+            )
+
+        def finish(g):
+            result = results.tile([P, TILES, D], F32)
+            for b in range(BANKS):
+                first = BANK_TILES * b
+                pair = slice(first, first + BANK_TILES)
+                for j in range(first, first + BANK_TILES):
+                    nc.scalar.activation(
+                        out=result[:, j, :],
+                        in_=z_of[g][:, j, :],
+                        func=ACT.Identity,
+                        scale=rstd2_of[g][:, j : j + 1],
+                        bias=shift_of[g][:, j : j + 1],
+                    )
+                nc.sync.dma_start(out=out_groups[g][:, pair, :], in_=result[:, pair, :])
+
+        def run(stage, g, *bank):
+            if 0 <= g < GROUPS:
+                stage(g, *bank)
+
+        def step(s):
+            run(first_moments, s)
+            run(quantise, s + 1)
+            run(multiply, s + 1)
+            run(turn, s + 3)
+            run(regroup, s + 2, 0)
+            run(second_root, s - 1)
+            run(regroup, s + 2, 1)
+            run(first_root, s)
+            run(second_shift, s - 1)
+            run(finish, s - 1)
+            run(centre, s)
+            run(residual, s)
+            run(second_squares, s)
+
+        first_step = -3
+        step(first_step)
+        quantise_decoder()
+        make_gain()
+        for s in range(first_step + 1, GROUPS + 1):
+            step(s)

@@ -43,7 +43,7 @@ def tile_bdhlayer_pc_t_kernel(tc, xy_sparse, decoder, x, scale, running_activity
         inputs = ctx.enter_context(tc.tile_pool(name="inputs", bufs=GROUPS))
         quant = ctx.enter_context(tc.tile_pool(name="quant", bufs=2))
         work = ctx.enter_context(tc.tile_pool(name="work", bufs=3))
-        results = ctx.enter_context(tc.tile_pool(name="results", bufs=4))
+        results = ctx.enter_context(tc.tile_pool(name="results", bufs=GROUPS))
         stats = ctx.enter_context(tc.tile_pool(name="stats", bufs=3))
         turned_pool = ctx.enter_context(tc.psum_pool(name="turned", bufs=2 * BANKS))
         product_pool = ctx.enter_context(tc.psum_pool(name="product", bufs=2 * BANKS))

@@ -41,10 +41,10 @@ def tile_bdhlayer_pc_t_kernel(tc, xy_sparse, decoder, x, scale, running_activity
     with ExitStack() as ctx:
         const = ctx.enter_context(tc.tile_pool(name="const", bufs=1))
         inputs = ctx.enter_context(tc.tile_pool(name="inputs", bufs=GROUPS))
-        quant = ctx.enter_context(tc.tile_pool(name="quant", bufs=2))
-        work = ctx.enter_context(tc.tile_pool(name="work", bufs=3))
+        quant = ctx.enter_context(tc.tile_pool(name="quant", bufs=3))
+        work = ctx.enter_context(tc.tile_pool(name="work", bufs=4))
         results = ctx.enter_context(tc.tile_pool(name="results", bufs=GROUPS))
-        stats = ctx.enter_context(tc.tile_pool(name="stats", bufs=3))
+        stats = ctx.enter_context(tc.tile_pool(name="stats", bufs=5))
         turned_pool = ctx.enter_context(tc.psum_pool(name="turned", bufs=2 * BANKS))
         product_pool = ctx.enter_context(tc.psum_pool(name="product", bufs=2 * BANKS))
 
@@ -171,13 +171,43 @@ def tile_bdhlayer_pc_t_kernel(tc, xy_sparse, decoder, x, scale, running_activity
                         stop=True,
                     )
 
+        def scalar_takes_moments(g):
+            return g < 3 or g in (6, 10)
+
         def first_moments(g):
             moments = stats.tile([P, TILES, 3], F32)
             moments_of[g] = moments
             for b in range(BANKS):
+                if b == 1 and scalar_takes_moments(g):
+                    continue
                 nc.vector.bn_stats(
                     out=moments[:, BANK_TILES * b : BANK_TILES * (b + 1), :].rearrange("p a m -> p (a m)"),
                     in_=products_of[g][b][:].rearrange("p a d -> p d a"),
+                )
+
+        def first_moments_scalar(g):
+            if not scalar_takes_moments(g):
+                return
+            moments = moments_of[g]
+            terms = work.tile([P, 2, BANK_TILES, D], BF16)
+            for a in range(BANK_TILES):
+                j = BANK_TILES + a
+                nc.scalar.activation(
+                    out=terms[:, 0, a, :],
+                    in_=products_of[g][1][:, a, :],
+                    func=ACT.Identity,
+                    scale=1.0 / float(D),
+                    accum_out=moments[:, j, 1:2],
+                )
+            for a in range(BANK_TILES):
+                j = BANK_TILES + a
+                nc.scalar.activation(
+                    out=terms[:, 1, a, :],
+                    in_=products_of[g][1][:, a, :],
+                    func=ACT.Square,
+                    scale=-1.0,
+                    bias=moments[:, j, 1:2],
+                    accum_out=moments[:, j, 2:3],
                 )
 
         def first_root(g):
@@ -220,42 +250,59 @@ def tile_bdhlayer_pc_t_kernel(tc, xy_sparse, decoder, x, scale, running_activity
                     accum_out=z_sum[:, j : j + 1],
                 )
 
-        def second_squares(g):
-            squares = work.tile([P, TILES, D], BF16)
-            square_sum = stats.tile([P, TILES], F32)
-            square_sum_of[g] = square_sum
-            for j in range(TILES):
-                nc.scalar.activation(
-                    out=squares[:, j, :],
-                    in_=z_of[g][:, j, :],
-                    func=ACT.Square,
-                    scale=-float(D),
-                    bias=z_sum_of[g][:, j : j + 1],
-                    accum_out=square_sum[:, j : j + 1],
-                )
-
-        def second_root(g):
-            rstd2 = stats.tile([P, TILES], F32)
-            rstd2_of[g] = rstd2
+        def squares_of_tile(g, j, squares, square_sum):
             nc.scalar.activation(
-                out=rstd2[:],
-                in_=square_sum_of[g][:],
+                out=squares[:, j, :],
+                in_=z_of[g][:, j, :],
+                func=ACT.Square,
+                scale=-float(D),
+                bias=z_sum_of[g][:, j : j + 1],
+                accum_out=square_sum[:, j : j + 1],
+            )
+
+        def root_of_squares(rstd2, square_sum):
+            nc.scalar.activation(
+                out=rstd2,
+                in_=square_sum,
                 func=ACT.Abs_reciprocal_sqrt,
                 scale=1.0 / float(D * D * D),
                 bias=eps_ln[:, 0:1],
             )
 
+        def shift_of_sums(shift, z_sum, rstd2):
+            nc.vector.scalar_tensor_tensor(
+                out=shift, in0=z_sum, scalar=-1.0 / float(D), in1=rstd2, op0=ALU.mult, op1=ALU.mult
+            )
+
+        def second_squares(g):
+            squares = work.tile([P, TILES, D], BF16)
+            square_sum = stats.tile([P, TILES], F32)
+            square_sum_of[g] = square_sum
+            for j in range(TILES):
+                squares_of_tile(g, j, squares, square_sum)
+
+        def second_root(g):
+            rstd2 = stats.tile([P, TILES], F32)
+            rstd2_of[g] = rstd2
+            root_of_squares(rstd2[:], square_sum_of[g][:])
+
         def second_shift(g):
             shift = stats.tile([P, TILES], F32)
             shift_of[g] = shift
-            nc.vector.scalar_tensor_tensor(
-                out=shift[:],
-                in0=z_sum_of[g][:],
-                scalar=-1.0 / float(D),
-                in1=rstd2_of[g][:],
-                op0=ALU.mult,
-                op1=ALU.mult,
-            )
+            shift_of_sums(shift[:], z_sum_of[g][:], rstd2_of[g][:])
+
+        def finish_on_vector(g):
+            result = results.tile([P, TILES, D], F32)
+            for j in range(TILES):
+                nc.vector.tensor_scalar(
+                    out=result[:, j, :],
+                    in0=z_of[g][:, j, :],
+                    scalar1=rstd2_of[g][:, j : j + 1],
+                    scalar2=shift_of[g][:, j : j + 1],
+                    op0=ALU.mult,
+                    op1=ALU.add,
+                )
+            nc.sync.dma_start(out=out_groups[g], in_=result[:])
 
         def finish(g):
             result = results.tile([P, TILES, D], F32)
@@ -272,28 +319,62 @@ def tile_bdhlayer_pc_t_kernel(tc, xy_sparse, decoder, x, scale, running_activity
                     )
                 nc.sync.dma_start(out=out_groups[g][:, pair, :], in_=result[:, pair, :])
 
-        def run(stage, g, *bank):
+        def second_norm_of_last(g):
+            result = results.tile([P, TILES, D], F32)
+            squares = work.tile([P, TILES, D], BF16)
+            square_sum = stats.tile([P, TILES], F32)
+            rstd2 = stats.tile([P, TILES], F32)
+            shift = stats.tile([P, TILES], F32)
+            for b in range(BANKS):
+                first = BANK_TILES * b
+                pair = slice(first, first + BANK_TILES)
+                for j in range(first, first + BANK_TILES):
+                    squares_of_tile(g, j, squares, square_sum)
+                root_of_squares(rstd2[:, pair], square_sum[:, pair])
+                shift_of_sums(shift[:, pair], z_sum_of[g][:, pair], rstd2[:, pair])
+                nc.vector.tensor_scalar(
+                    out=result[:, first, :],
+                    in0=z_of[g][:, first, :],
+                    scalar1=rstd2[:, first : first + 1],
+                    scalar2=shift[:, first : first + 1],
+                    op0=ALU.mult,
+                    op1=ALU.add,
+                )
+                nc.scalar.activation(
+                    out=result[:, first + 1, :],
+                    in_=z_of[g][:, first + 1, :],
+                    func=ACT.Identity,
+                    scale=rstd2[:, first + 1 : first + 2],
+                    bias=shift[:, first + 1 : first + 2],
+                )
+                nc.sync.dma_start(out=out_groups[g][:, pair, :], in_=result[:, pair, :])
+
+        def run(stage, g, *more):
             if 0 <= g < GROUPS:
-                stage(g, *bank)
+                stage(g, *more)
 
         def step(s):
-            run(first_moments, s)
-            run(quantise, s + 1)
-            run(multiply, s + 1)
-            run(turn, s + 3)
-            run(regroup, s + 2, 0)
+            run(second_squares, s - 1)
             run(second_root, s - 1)
-            run(regroup, s + 2, 1)
-            run(first_root, s)
-            run(second_shift, s - 1)
-            run(finish, s - 1)
+            run(second_shift, s - 2)
+            run(multiply, s + 1)
             run(centre, s)
+            run(first_moments, s + 1)
+            run(first_moments_scalar, s + 1)
+            run(first_root, s + 1)
+            run(regroup, s + 3, 0)
+            run(regroup, s + 3, 1)
+            run(finish, s - 2)
             run(residual, s)
-            run(second_squares, s)
+            run(turn, s + 4)
+            run(quantise, s + 2)
 
-        first_step = -3
+        first_step = -4
         step(first_step)
         quantise_decoder()
         make_gain()
-        for s in range(first_step + 1, GROUPS + 1):
+        for s in range(first_step + 1, GROUPS):
             step(s)
+        second_shift(GROUPS - 2)
+        finish_on_vector(GROUPS - 2)
+        second_norm_of_last(GROUPS - 1)

@@ -172,7 +172,7 @@ def tile_bdhlayer_pc_t_kernel(tc, xy_sparse, decoder, x, scale, running_activity
                     )
 
         def scalar_takes_moments(g):
-            return g < 3 or g in (6, 10)
+            return g < 3 or g % 2 == 0
 
         def first_moments(g):
             moments = stats.tile([P, TILES, 3], F32)
@@ -306,18 +306,24 @@ def tile_bdhlayer_pc_t_kernel(tc, xy_sparse, decoder, x, scale, running_activity
 
         def finish(g):
             result = results.tile([P, TILES, D], F32)
-            for b in range(BANKS):
-                first = BANK_TILES * b
-                pair = slice(first, first + BANK_TILES)
-                for j in range(first, first + BANK_TILES):
-                    nc.scalar.activation(
-                        out=result[:, j, :],
-                        in_=z_of[g][:, j, :],
-                        func=ACT.Identity,
-                        scale=rstd2_of[g][:, j : j + 1],
-                        bias=shift_of[g][:, j : j + 1],
-                    )
-                nc.sync.dma_start(out=out_groups[g][:, pair, :], in_=result[:, pair, :])
+            for j in range(BANK_TILES, TILES):
+                nc.gpsimd.tensor_scalar(
+                    out=result[:, j, :],
+                    in0=z_of[g][:, j, :],
+                    scalar1=rstd2_of[g][:, j : j + 1],
+                    scalar2=shift_of[g][:, j : j + 1],
+                    op0=ALU.mult,
+                    op1=ALU.add,
+                )
+            for j in range(BANK_TILES):
+                nc.scalar.activation(
+                    out=result[:, j, :],
+                    in_=z_of[g][:, j, :],
+                    func=ACT.Identity,
+                    scale=rstd2_of[g][:, j : j + 1],
+                    bias=shift_of[g][:, j : j + 1],
+                )
+            nc.sync.dma_start(out=out_groups[g], in_=result[:])
 
         def second_norm_of_last(g):
             result = results.tile([P, TILES, D], F32)
@@ -362,19 +368,28 @@ def tile_bdhlayer_pc_t_kernel(tc, xy_sparse, decoder, x, scale, running_activity
             run(first_moments, s + 1)
             run(first_moments_scalar, s + 1)
             run(first_root, s + 1)
+            run(residual, s)
+            run(turn, s + 4)
             run(regroup, s + 3, 0)
             run(regroup, s + 3, 1)
             run(finish, s - 2)
-            run(residual, s)
-            run(turn, s + 4)
             run(quantise, s + 2)
 
         first_step = -4
         step(first_step)
         quantise_decoder()
         make_gain()
-        for s in range(first_step + 1, GROUPS):
+        compute = {
+            mybir.EngineType.PE,
+            mybir.EngineType.Activation,
+            mybir.EngineType.DVE,
+            mybir.EngineType.Pool,
+        }
+        for s in range(first_step + 1, 0):
             step(s)
-        second_shift(GROUPS - 2)
-        finish_on_vector(GROUPS - 2)
-        second_norm_of_last(GROUPS - 1)
+        with tc.manual_schedule(engines=compute):
+            for s in range(GROUPS):
+                step(s)
+            second_shift(GROUPS - 2)
+            finish_on_vector(GROUPS - 2)
+            second_norm_of_last(GROUPS - 1)

@@ -53,21 +53,34 @@ def tile_bdhlayer_pc_t_kernel(tc, xy_sparse, decoder, x, scale, running_activity
         rows = const.tile([P, 2, D], BF16)
         dec_raw = const.tile([P, PACK, D], BF16)
         nc.vector.memset(rows[:], 0.0)
-        for g in range(GROUPS):
+
+        nc.scalar.dma_start(out=rows[0:1, 0, :], in_=scale.rearrange("(o d) -> o d", o=1))
+        nc.scalar.dma_start(out=rows[0:1, 1, :], in_=running_activity.rearrange("(o d) -> o d", o=1))
+
+        def load_xy(g, tiles):
             xy_sb = inputs.tile([P, TILES, HEADS, HEAD_DIM], BF16)
-            for h in range(HEADS):
-                nc.sync.dma_start(out=xy_sb[:, :, h, :], in_=xy_groups[g, h])
+            for first in range(0, TILES, tiles):
+                for h in range(HEADS):
+                    nc.sync.dma_start(
+                        out=xy_sb[:, first : first + tiles, h, :],
+                        in_=xy_groups[g, h][:, first : first + tiles, :],
+                    )
             xy_tiles.append(xy_sb)
-            if g == 0:
-                nc.sync.dma_start(out=rows[0:1, 0, :], in_=scale.rearrange("(o d) -> o d", o=1))
-                nc.sync.dma_start(out=rows[0:1, 1, :], in_=running_activity.rearrange("(o d) -> o d", o=1))
-                nc.sync.dma_start(
-                    out=dec_raw[:].rearrange("p t d -> p (t d)"),
-                    in_=decoder.rearrange("(p t) d -> p (t d)", t=PACK),
-                )
+
+        def load_x(g):
             x_sb = inputs.tile([P, TILES, D], BF16)
             nc.sync.dma_start(out=x_sb[:].rearrange("p j d -> p (j d)"), in_=x_groups[g])
             x_tiles.append(x_sb)
+
+        load_xy(0, BANK_TILES)
+        nc.sync.dma_start(
+            out=dec_raw[:].rearrange("p t d -> p (t d)"),
+            in_=decoder.rearrange("(p t) d -> p (t d)", t=PACK),
+        )
+        for g in range(GROUPS):
+            if g + 1 < GROUPS:
+                load_xy(g + 1, TILES)
+            load_x(g)
 
         ident = const.tile([P, P], F32)
         masks.make_identity(nc, ident[:])
@@ -75,6 +88,8 @@ def tile_bdhlayer_pc_t_kernel(tc, xy_sparse, decoder, x, scale, running_activity
         nc.vector.memset(ones[:], 1.0)
         eps_ln = const.tile([P, 1], F32)
         nc.vector.memset(eps_ln[:], EPS_LN)
+        table = const.tile([P, 1], F32)
+        nc.scalar.activation(out=table[:], in_=eps_ln[:], func=ACT.Abs_reciprocal_sqrt)
         eps_activity = const.tile([P, 1], F32)
         nc.vector.memset(eps_activity[:], EPS_ACTIVITY / TARGET_ACTIVITY)
         dec_codes = const.tile([P, D], U32, align_bytes=64)
@@ -172,7 +187,7 @@ def tile_bdhlayer_pc_t_kernel(tc, xy_sparse, decoder, x, scale, running_activity
                     )
 
         def scalar_takes_moments(g):
-            return g < 3 or g % 2 == 0
+            return g < 3 or g % 3 != 0
 
         def first_moments(g):
             moments = stats.tile([P, TILES, 3], F32)
@@ -306,7 +321,8 @@ def tile_bdhlayer_pc_t_kernel(tc, xy_sparse, decoder, x, scale, running_activity
 
         def finish(g):
             result = results.tile([P, TILES, D], F32)
-            for j in range(BANK_TILES, TILES):
+            scalar_tiles = BANK_TILES if scalar_takes_moments(g + 3) else 0
+            for j in range(scalar_tiles, TILES):
                 nc.gpsimd.tensor_scalar(
                     out=result[:, j, :],
                     in0=z_of[g][:, j, :],
@@ -315,7 +331,7 @@ def tile_bdhlayer_pc_t_kernel(tc, xy_sparse, decoder, x, scale, running_activity
                     op0=ALU.mult,
                     op1=ALU.add,
                 )
-            for j in range(BANK_TILES):
+            for j in range(scalar_tiles):
                 nc.scalar.activation(
                     out=result[:, j, :],
                     in_=z_of[g][:, j, :],
@@ -328,16 +344,37 @@ def tile_bdhlayer_pc_t_kernel(tc, xy_sparse, decoder, x, scale, running_activity
         def second_norm_of_last(g):
             result = results.tile([P, TILES, D], F32)
             squares = work.tile([P, TILES, D], BF16)
-            square_sum = stats.tile([P, TILES], F32)
+            square_sum = stats.tile([P, BANK_TILES], F32)
+            moments = stats.tile([P, BANK_TILES, 3], F32)
             rstd2 = stats.tile([P, TILES], F32)
             shift = stats.tile([P, TILES], F32)
+            pairs = [slice(BANK_TILES * b, BANK_TILES * (b + 1)) for b in range(BANKS)]
+            for j in range(BANK_TILES):
+                squares_of_tile(g, j, squares, square_sum)
+            root_of_squares(rstd2[:, pairs[0]], square_sum[:])
+            nc.vector.bn_stats(
+                out=moments[:].rearrange("p a m -> p (a m)"),
+                in_=z_of[g][:, pairs[1], :].rearrange("p a d -> p d a"),
+            )
+            finish_on_vector(GROUPS - 2)
+            nc.scalar.activation(
+                out=rstd2[:, pairs[1]],
+                in_=moments[:, :, 2],
+                func=ACT.Abs_reciprocal_sqrt,
+                scale=1.0 / float(D),
+                bias=eps_ln[:, 0:1],
+            )
+            shift_of_sums(shift[:, pairs[0]], z_sum_of[g][:, pairs[0]], rstd2[:, pairs[0]])
+            nc.vector.scalar_tensor_tensor(
+                out=shift[:, pairs[1]],
+                in0=moments[:, :, 1],
+                scalar=-1.0,
+                in1=rstd2[:, pairs[1]],
+                op0=ALU.mult,
+                op1=ALU.mult,
+            )
             for b in range(BANKS):
                 first = BANK_TILES * b
-                pair = slice(first, first + BANK_TILES)
-                for j in range(first, first + BANK_TILES):
-                    squares_of_tile(g, j, squares, square_sum)
-                root_of_squares(rstd2[:, pair], square_sum[:, pair])
-                shift_of_sums(shift[:, pair], z_sum_of[g][:, pair], rstd2[:, pair])
                 nc.vector.tensor_scalar(
                     out=result[:, first, :],
                     in0=z_of[g][:, first, :],
@@ -353,7 +390,7 @@ def tile_bdhlayer_pc_t_kernel(tc, xy_sparse, decoder, x, scale, running_activity
                     scale=rstd2[:, first + 1 : first + 2],
                     bias=shift[:, first + 1 : first + 2],
                 )
-                nc.sync.dma_start(out=out_groups[g][:, pair, :], in_=result[:, pair, :])
+                nc.sync.dma_start(out=out_groups[g][:, pairs[b], :], in_=result[:, pairs[b], :])
 
         def run(stage, g, *more):
             if 0 <= g < GROUPS:
@@ -363,33 +400,46 @@ def tile_bdhlayer_pc_t_kernel(tc, xy_sparse, decoder, x, scale, running_activity
             run(second_squares, s - 1)
             run(second_root, s - 1)
             run(second_shift, s - 2)
-            run(multiply, s + 1)
             run(centre, s)
             run(first_moments, s + 1)
             run(first_moments_scalar, s + 1)
-            run(first_root, s + 1)
             run(residual, s)
             run(turn, s + 4)
             run(regroup, s + 3, 0)
             run(regroup, s + 3, 1)
+            run(first_root, s + 1)
             run(finish, s - 2)
             run(quantise, s + 2)
+            run(multiply, s + 2)
 
-        first_step = -4
-        step(first_step)
-        quantise_decoder()
-        make_gain()
+        with tc.manual_schedule(engines={mybir.EngineType.PE}):
+            turn(0)
+            turn(1)
+            make_gain()
+            quantise_decoder()
+            regroup(0, 0)
+            regroup(0, 1)
+            quantise(0)
+            multiply(0)
+            turn(2)
+            regroup(1, 0)
+            regroup(1, 1)
+            first_moments(0)
+            first_moments_scalar(0)
+            first_root(0)
+            quantise(1)
+            multiply(1)
+            turn(3)
+            regroup(2, 0)
+            regroup(2, 1)
         compute = {
             mybir.EngineType.PE,
             mybir.EngineType.Activation,
             mybir.EngineType.DVE,
             mybir.EngineType.Pool,
         }
-        for s in range(first_step + 1, 0):
-            step(s)
         with tc.manual_schedule(engines=compute):
             for s in range(GROUPS):
                 step(s)
             second_shift(GROUPS - 2)
-            finish_on_vector(GROUPS - 2)
             second_norm_of_last(GROUPS - 1)

@@ -187,7 +187,7 @@ def tile_bdhlayer_pc_t_kernel(tc, xy_sparse, decoder, x, scale, running_activity
                     )
 
         def scalar_takes_moments(g):
-            return g < 3 or g % 3 != 0
+            return g < 3 or (g % 4 != 0 and g < GROUPS - 1)
 
         def first_moments(g):
             moments = stats.tile([P, TILES, 3], F32)
@@ -256,13 +256,13 @@ def tile_bdhlayer_pc_t_kernel(tc, xy_sparse, decoder, x, scale, running_activity
             z_sum_of[g] = z_sum
             for j in range(TILES):
                 nc.vector.scalar_tensor_tensor(
-                    out=z[:, j, :],
+                    out=z_of[g][:, j, :],
                     in0=centred_of[g][:, j, :],
                     scalar=rstd_of[g][:, j : j + 1],
                     in1=x_tiles[g][:, j, :],
                     op0=ALU.mult,
                     op1=ALU.add,
-                    accum_out=z_sum[:, j : j + 1],
+                    accum_out=z_sum_of[g][:, j : j + 1],
                 )
 
         def squares_of_tile(g, j, squares, square_sum):
@@ -306,57 +306,53 @@ def tile_bdhlayer_pc_t_kernel(tc, xy_sparse, decoder, x, scale, running_activity
             shift_of[g] = shift
             shift_of_sums(shift[:], z_sum_of[g][:], rstd2_of[g][:])
 
-        def finish_on_vector(g):
-            result = results.tile([P, TILES, D], F32)
-            for j in range(TILES):
-                nc.vector.tensor_scalar(
-                    out=result[:, j, :],
-                    in0=z_of[g][:, j, :],
-                    scalar1=rstd2_of[g][:, j : j + 1],
-                    scalar2=shift_of[g][:, j : j + 1],
-                    op0=ALU.mult,
-                    op1=ALU.add,
+        def finish_tile(engine, g, j, result, rstd2, shift):
+            scale = rstd2[:, j : j + 1]
+            bias = shift[:, j : j + 1]
+            if engine is nc.scalar:
+                nc.scalar.activation(
+                    out=result[:, j, :], in_=z_of[g][:, j, :], func=ACT.Identity, scale=scale, bias=bias
                 )
-            nc.sync.dma_start(out=out_groups[g], in_=result[:])
+            else:
+                engine.tensor_scalar(
+                    out=result[:, j, :], in0=z_of[g][:, j, :], scalar1=scale, scalar2=bias, op0=ALU.mult, op1=ALU.add
+                )
 
         def finish(g):
             result = results.tile([P, TILES, D], F32)
-            scalar_tiles = BANK_TILES if scalar_takes_moments(g + 3) else 0
+            scalar_tiles = 1 if scalar_takes_moments(g + 3) else 0
             for j in range(scalar_tiles, TILES):
-                nc.gpsimd.tensor_scalar(
-                    out=result[:, j, :],
-                    in0=z_of[g][:, j, :],
-                    scalar1=rstd2_of[g][:, j : j + 1],
-                    scalar2=shift_of[g][:, j : j + 1],
-                    op0=ALU.mult,
-                    op1=ALU.add,
-                )
+                finish_tile(nc.gpsimd, g, j, result, rstd2_of[g], shift_of[g])
             for j in range(scalar_tiles):
-                nc.scalar.activation(
-                    out=result[:, j, :],
-                    in_=z_of[g][:, j, :],
-                    func=ACT.Identity,
-                    scale=rstd2_of[g][:, j : j + 1],
-                    bias=shift_of[g][:, j : j + 1],
-                )
+                finish_tile(nc.scalar, g, j, result, rstd2_of[g], shift_of[g])
             nc.sync.dma_start(out=out_groups[g], in_=result[:])
 
+        def finish_pair(g, b, engines, result, rstd2, shift):
+            pair = slice(BANK_TILES * b, BANK_TILES * (b + 1))
+            for a in range(BANK_TILES):
+                finish_tile(engines[a], g, BANK_TILES * b + a, result, rstd2, shift)
+            nc.sync.dma_start(out=out_groups[g][:, pair, :], in_=result[:, pair, :])
+
+        def finish_by_pairs(g, engines):
+            result = results.tile([P, TILES, D], F32)
+            for b in range(BANKS):
+                finish_pair(g, b, [engines[b]] * BANK_TILES, result, rstd2_of[g], shift_of[g])
+
         def second_norm_of_last(g):
+            pairs = [slice(BANK_TILES * b, BANK_TILES * (b + 1)) for b in range(BANKS)]
             result = results.tile([P, TILES, D], F32)
             squares = work.tile([P, TILES, D], BF16)
             square_sum = stats.tile([P, BANK_TILES], F32)
             moments = stats.tile([P, BANK_TILES, 3], F32)
             rstd2 = stats.tile([P, TILES], F32)
             shift = stats.tile([P, TILES], F32)
-            pairs = [slice(BANK_TILES * b, BANK_TILES * (b + 1)) for b in range(BANKS)]
-            for j in range(BANK_TILES):
-                squares_of_tile(g, j, squares, square_sum)
-            root_of_squares(rstd2[:, pairs[0]], square_sum[:])
             nc.vector.bn_stats(
                 out=moments[:].rearrange("p a m -> p (a m)"),
                 in_=z_of[g][:, pairs[1], :].rearrange("p a d -> p d a"),
             )
-            finish_on_vector(GROUPS - 2)
+            for j in range(BANK_TILES):
+                squares_of_tile(g, j, squares, square_sum)
+            root_of_squares(rstd2[:, pairs[0]], square_sum[:])
             nc.scalar.activation(
                 out=rstd2[:, pairs[1]],
                 in_=moments[:, :, 2],
@@ -365,6 +361,7 @@ def tile_bdhlayer_pc_t_kernel(tc, xy_sparse, decoder, x, scale, running_activity
                 bias=eps_ln[:, 0:1],
             )
             shift_of_sums(shift[:, pairs[0]], z_sum_of[g][:, pairs[0]], rstd2[:, pairs[0]])
+            finish_pair(g, 0, [nc.vector, nc.scalar], result, rstd2, shift)
             nc.vector.scalar_tensor_tensor(
                 out=shift[:, pairs[1]],
                 in0=moments[:, :, 1],
@@ -373,24 +370,7 @@ def tile_bdhlayer_pc_t_kernel(tc, xy_sparse, decoder, x, scale, running_activity
                 op0=ALU.mult,
                 op1=ALU.mult,
             )
-            for b in range(BANKS):
-                first = BANK_TILES * b
-                nc.vector.tensor_scalar(
-                    out=result[:, first, :],
-                    in0=z_of[g][:, first, :],
-                    scalar1=rstd2[:, first : first + 1],
-                    scalar2=shift[:, first : first + 1],
-                    op0=ALU.mult,
-                    op1=ALU.add,
-                )
-                nc.scalar.activation(
-                    out=result[:, first + 1, :],
-                    in_=z_of[g][:, first + 1, :],
-                    func=ACT.Identity,
-                    scale=rstd2[:, first + 1 : first + 2],
-                    bias=shift[:, first + 1 : first + 2],
-                )
-                nc.sync.dma_start(out=out_groups[g][:, pairs[b], :], in_=result[:, pairs[b], :])
+            finish_pair(g, 1, [nc.vector, nc.scalar], result, rstd2, shift)
 
         def run(stage, g, *more):
             if 0 <= g < GROUPS:
@@ -439,7 +419,26 @@ def tile_bdhlayer_pc_t_kernel(tc, xy_sparse, decoder, x, scale, running_activity
             mybir.EngineType.Pool,
         }
         with tc.manual_schedule(engines=compute):
-            for s in range(GROUPS):
+            last = GROUPS - 1
+            for s in range(last - 1):
                 step(s)
-            second_shift(GROUPS - 2)
-            second_norm_of_last(GROUPS - 1)
+
+            second_squares(last - 2)
+            second_root(last - 2)
+            second_shift(last - 3)
+            centre(last - 1)
+            first_moments(last)
+            first_moments_scalar(last)
+            first_root(last)
+            finish(last - 3)
+            second_shift(last - 2)
+            residual(last - 1)
+            finish_by_pairs(last - 2, [nc.scalar, nc.vector])
+
+            second_squares(last - 1)
+            second_root(last - 1)
+            centre(last)
+            second_shift(last - 1)
+            residual(last)
+            finish_by_pairs(last - 1, [nc.scalar, nc.scalar])
+            second_norm_of_last(last)

@@ -187,7 +187,7 @@ def tile_bdhlayer_pc_t_kernel(tc, xy_sparse, decoder, x, scale, running_activity
                     )
 
         def scalar_takes_moments(g):
-            return g < 3 or (g % 4 != 0 and g < GROUPS - 1)
+            return g < 3 or g % 3 != 0
 
         def first_moments(g):
             moments = stats.tile([P, TILES, 3], F32)

@@ -320,7 +320,7 @@ def tile_bdhlayer_pc_t_kernel(tc, xy_sparse, decoder, x, scale, running_activity
 
         def finish(g):
             result = results.tile([P, TILES, D], F32)
-            scalar_tiles = 1 if scalar_takes_moments(g + 3) else 0
+            scalar_tiles = 2 if scalar_takes_moments(g + 3) else 1
             for j in range(scalar_tiles, TILES):
                 finish_tile(nc.gpsimd, g, j, result, rstd2_of[g], shift_of[g])
             for j in range(scalar_tiles):

from contextlib import ExitStack

import concourse.masks as masks
import concourse.mybir as mybir

F32 = mybir.dt.float32
BF16 = mybir.dt.bfloat16
U32 = mybir.dt.uint32
U8 = mybir.dt.uint8
FP8X4 = mybir.dt.float8_e4m3fn_x4
ALU = mybir.AluOpType
ACT = mybir.ActivationFunctionType

P = 128
HEADS = 2
HEAD_DIM = 256
K = HEADS * HEAD_DIM
PACK = 4
WORDS = K // 2
PAIRS = PACK // 2
D = 256
T = 8192
TILES = 4
BANK_TILES = 2
BANKS = TILES // BANK_TILES
GROUPS = T // (P * TILES)
EPS_LN = 1e-5
EPS_ACTIVITY = 1e-6
TARGET_ACTIVITY = 0.1

FLOPS = 2 * T * K * D


def tile_bdhlayer_pc_t_kernel(tc, xy_sparse, decoder, x, scale, running_activity, out):
    nc = tc.nc

    xy_groups = xy_sparse[0].rearrange("h (g p j) n -> g h p j n", p=P, j=TILES)
    x_groups = x.flatten_outer_dims().rearrange("(g p j) d -> g p (j d)", p=P, j=TILES)
    out_groups = out.flatten_outer_dims().rearrange("(g p j) d -> g p j d", p=P, j=TILES)

    with ExitStack() as ctx:
        const = ctx.enter_context(tc.tile_pool(name="const", bufs=1))
        inputs = ctx.enter_context(tc.tile_pool(name="inputs", bufs=GROUPS))
        quant = ctx.enter_context(tc.tile_pool(name="quant", bufs=3))
        work = ctx.enter_context(tc.tile_pool(name="work", bufs=4))
        results = ctx.enter_context(tc.tile_pool(name="results", bufs=GROUPS))
        stats = ctx.enter_context(tc.tile_pool(name="stats", bufs=5))
        turned_pool = ctx.enter_context(tc.psum_pool(name="turned", bufs=2 * BANKS))
        product_pool = ctx.enter_context(tc.psum_pool(name="product", bufs=2 * BANKS))

        xy_tiles = []
        x_tiles = []
        rows = const.tile([P, 2, D], BF16)
        dec_raw = const.tile([P, PACK, D], BF16)
        nc.vector.memset(rows[:], 0.0)

        nc.scalar.dma_start(out=rows[0:1, 0, :], in_=scale.rearrange("(o d) -> o d", o=1))
        nc.scalar.dma_start(out=rows[0:1, 1, :], in_=running_activity.rearrange("(o d) -> o d", o=1))

        def load_xy(g, tiles):
            xy_sb = inputs.tile([P, TILES, HEADS, HEAD_DIM], BF16)
            for first in range(0, TILES, tiles):
                for h in range(HEADS):
                    nc.sync.dma_start(
                        out=xy_sb[:, first : first + tiles, h, :],
                        in_=xy_groups[g, h][:, first : first + tiles, :],
                    )
            xy_tiles.append(xy_sb)

        def load_x(g):
            x_sb = inputs.tile([P, TILES, D], BF16)
            nc.sync.dma_start(out=x_sb[:].rearrange("p j d -> p (j d)"), in_=x_groups[g])
            x_tiles.append(x_sb)

        load_xy(0, BANK_TILES)
        nc.sync.dma_start(
            out=dec_raw[:].rearrange("p t d -> p (t d)"),
            in_=decoder.rearrange("(p t) d -> p (t d)", t=PACK),
        )
        for g in range(GROUPS):
            if g + 1 < GROUPS:
                load_xy(g + 1, TILES)
            load_x(g)

        ident = const.tile([P, P], F32)
        masks.make_identity(nc, ident[:])
        ones = const.tile([P, P], BF16)
        nc.vector.memset(ones[:], 1.0)
        eps_ln = const.tile([P, 1], F32)
        nc.vector.memset(eps_ln[:], EPS_LN)
        table = const.tile([P, 1], F32)
        nc.scalar.activation(out=table[:], in_=eps_ln[:], func=ACT.Abs_reciprocal_sqrt)
        eps_activity = const.tile([P, 1], F32)
        nc.vector.memset(eps_activity[:], EPS_ACTIVITY / TARGET_ACTIVITY)
        dec_codes = const.tile([P, D], U32, align_bytes=64)
        dec_scales = const.tile([P, D], U8, align_bytes=64)
        gain = const.tile([P, D], F32)

        def quantise_decoder():
            dec_grouped = const.tile([P, D, PACK], BF16, align_bytes=64)
            nc.vector.tensor_copy(out=dec_grouped[:], in_=dec_raw[:].rearrange("p t d -> p d t"))
            nc.vector.quantize_mx(
                out=dec_codes[:].bitcast(FP8X4),
                scales=dec_scales[:],
                in_=dec_grouped[:].rearrange("p d t -> p (d t)"),
            )

        def make_gain():
            spread = product_pool.tile([P, BANK_TILES, D], F32, tag="product")
            nc.tensor.matmul(
                spread[:].rearrange("p a d -> p (a d)"),
                lhsT=ones[:],
                rhs=rows[:].rearrange("p a d -> p (a d)"),
                start=True,
                stop=True,
            )
            regulation = const.tile([P, D], F32)
            nc.scalar.activation(
                out=regulation[:],
                in_=spread[:, 1, :],
                func=ACT.Abs_reciprocal_sqrt,
                scale=1.0 / TARGET_ACTIVITY,
                bias=eps_activity[:, 0:1],
            )
            nc.vector.tensor_tensor(out=gain[:], in0=regulation[:], in1=spread[:, 0, :], op=ALU.mult)

        turned_of = {}
        grouped_of = {}
        codes_of = {}
        scales_of = {}
        products_of = {}
        moments_of = {}
        rstd_of = {}
        centred_of = {}
        z_of = {}
        z_sum_of = {}
        square_sum_of = {}
        rstd2_of = {}
        shift_of = {}

        def turn(g):
            xy_words = xy_tiles[g][:].rearrange("p j h n -> p (j h n)").bitcast(F32)
            turned_of[g] = []
            for b in range(BANKS):
                turned = turned_pool.tile([P, BANK_TILES, PAIRS, P], F32)
                turned_of[g].append(turned)
                for a in range(BANK_TILES):
                    first = (BANK_TILES * b + a) * WORDS
                    for u in range(PAIRS):
                        words = slice(first + u, first + WORDS, PAIRS)
                        nc.tensor.transpose(turned[:, a, u, :], xy_words[:, words], ident[:])

        def regroup(g, b):
            if b == 0:
                grouped = quant.tile([P, BANKS, BANK_TILES * K], BF16, align_bytes=64)
                grouped_of[g] = grouped
            nc.scalar.copy(
                out=grouped_of[g][:, b, :].bitcast(F32).rearrange("p (a t u) -> p a t u", a=BANK_TILES, u=PAIRS),
                in_=turned_of[g][b][:].rearrange("p a u t -> p a t u"),
            )

        def quantise(g):
            codes = quant.tile([P, BANKS, BANK_TILES * P], U32, align_bytes=64)
            scales = quant.tile([P, BANKS, BANK_TILES * P], U8, align_bytes=64)
            codes_of[g] = codes
            scales_of[g] = scales
            for b in range(BANKS):
                nc.vector.quantize_mx(
                    out=codes[:, b, :].bitcast(FP8X4), scales=scales[:, b, :], in_=grouped_of[g][:, b, :]
                )

        def multiply(g):
            products_of[g] = []
            for b in range(BANKS):
                product = product_pool.tile([P, BANK_TILES, D], F32)
                products_of[g].append(product)
                for a in range(BANK_TILES):
                    tokens = slice(P * a, P * (a + 1))
                    nc.tensor.matmul_mx(
                        out=product[:, a, :],
                        lhsT=codes_of[g][:, b, tokens].bitcast(FP8X4),
                        lhsT_scale=scales_of[g][:, b, tokens],
                        rhs=dec_codes[:].bitcast(FP8X4),
                        rhs_scale=dec_scales[:],
                        start=True,
                        stop=True,
                    )

        def scalar_takes_moments(g):
            return g < 3 or g % 3 != 0

        def first_moments(g):
            moments = stats.tile([P, TILES, 3], F32)
            moments_of[g] = moments
            for b in range(BANKS):
                if b == 1 and scalar_takes_moments(g):
                    continue
                nc.vector.bn_stats(
                    out=moments[:, BANK_TILES * b : BANK_TILES * (b + 1), :].rearrange("p a m -> p (a m)"),
                    in_=products_of[g][b][:].rearrange("p a d -> p d a"),
                )

        def first_moments_scalar(g):
            if not scalar_takes_moments(g):
                return
            moments = moments_of[g]
            terms = work.tile([P, 2, BANK_TILES, D], BF16)
            for a in range(BANK_TILES):
                j = BANK_TILES + a
                nc.scalar.activation(
                    out=terms[:, 0, a, :],
                    in_=products_of[g][1][:, a, :],
                    func=ACT.Identity,
                    scale=1.0 / float(D),
                    accum_out=moments[:, j, 1:2],
                )
            for a in range(BANK_TILES):
                j = BANK_TILES + a
                nc.scalar.activation(
                    out=terms[:, 1, a, :],
                    in_=products_of[g][1][:, a, :],
                    func=ACT.Square,
                    scale=-1.0,
                    bias=moments[:, j, 1:2],
                    accum_out=moments[:, j, 2:3],
                )

        def first_root(g):
            rstd = stats.tile([P, TILES], F32)
            rstd_of[g] = rstd
            nc.scalar.activation(
                out=rstd[:],
                in_=moments_of[g][:, :, 2],
                func=ACT.Abs_reciprocal_sqrt,
                scale=1.0 / float(D),
                bias=eps_ln[:, 0:1],
            )

        def centre(g):
            centred = work.tile([P, TILES, D], F32)
            centred_of[g] = centred
            for j in range(TILES):
                nc.vector.scalar_tensor_tensor(
                    out=centred[:, j, :],
                    in0=products_of[g][j // BANK_TILES][:, j % BANK_TILES, :],
                    scalar=moments_of[g][:, j, 1:2],
                    in1=gain[:],
                    op0=ALU.subtract,
                    op1=ALU.mult,
                )

        def residual(g):
            z = work.tile([P, TILES, D], F32)
            z_sum = stats.tile([P, TILES], F32)
            z_of[g] = z
            z_sum_of[g] = z_sum
            for j in range(TILES):
                nc.vector.scalar_tensor_tensor(
                    out=z_of[g][:, j, :],
                    in0=centred_of[g][:, j, :],
                    scalar=rstd_of[g][:, j : j + 1],
                    in1=x_tiles[g][:, j, :],
                    op0=ALU.mult,
                    op1=ALU.add,
                    accum_out=z_sum_of[g][:, j : j + 1],
                )

        def squares_of_tile(g, j, squares, square_sum):
            nc.scalar.activation(
                out=squares[:, j, :],
                in_=z_of[g][:, j, :],
                func=ACT.Square,
                scale=-float(D),
                bias=z_sum_of[g][:, j : j + 1],
                accum_out=square_sum[:, j : j + 1],
            )

        def root_of_squares(rstd2, square_sum):
            nc.scalar.activation(
                out=rstd2,
                in_=square_sum,
                func=ACT.Abs_reciprocal_sqrt,
                scale=1.0 / float(D * D * D),
                bias=eps_ln[:, 0:1],
            )

        def shift_of_sums(shift, z_sum, rstd2):
            nc.vector.scalar_tensor_tensor(
                out=shift, in0=z_sum, scalar=-1.0 / float(D), in1=rstd2, op0=ALU.mult, op1=ALU.mult
            )

        def second_squares(g):
            squares = work.tile([P, TILES, D], BF16)
            square_sum = stats.tile([P, TILES], F32)
            square_sum_of[g] = square_sum
            for j in range(TILES):
                squares_of_tile(g, j, squares, square_sum)

        def second_root(g):
            rstd2 = stats.tile([P, TILES], F32)
            rstd2_of[g] = rstd2
            root_of_squares(rstd2[:], square_sum_of[g][:])

        def second_shift(g):
            shift = stats.tile([P, TILES], F32)
            shift_of[g] = shift
            shift_of_sums(shift[:], z_sum_of[g][:], rstd2_of[g][:])

        def finish_tile(engine, g, j, result, rstd2, shift):
            scale = rstd2[:, j : j + 1]
            bias = shift[:, j : j + 1]
            if engine is nc.scalar:
                nc.scalar.activation(
                    out=result[:, j, :], in_=z_of[g][:, j, :], func=ACT.Identity, scale=scale, bias=bias
                )
            else:
                engine.tensor_scalar(
                    out=result[:, j, :], in0=z_of[g][:, j, :], scalar1=scale, scalar2=bias, op0=ALU.mult, op1=ALU.add
                )

        def finish(g):
            result = results.tile([P, TILES, D], F32)
            scalar_tiles = 2 if scalar_takes_moments(g + 3) else 1
            for j in range(scalar_tiles, TILES):
                finish_tile(nc.gpsimd, g, j, result, rstd2_of[g], shift_of[g])
            for j in range(scalar_tiles):
                finish_tile(nc.scalar, g, j, result, rstd2_of[g], shift_of[g])
            nc.sync.dma_start(out=out_groups[g], in_=result[:])

        def finish_pair(g, b, engines, result, rstd2, shift):
            pair = slice(BANK_TILES * b, BANK_TILES * (b + 1))
            for a in range(BANK_TILES):
                finish_tile(engines[a], g, BANK_TILES * b + a, result, rstd2, shift)
            nc.sync.dma_start(out=out_groups[g][:, pair, :], in_=result[:, pair, :])

        def finish_by_pairs(g, engines):
            result = results.tile([P, TILES, D], F32)
            for b in range(BANKS):
                finish_pair(g, b, [engines[b]] * BANK_TILES, result, rstd2_of[g], shift_of[g])

        def second_norm_of_last(g):
            pairs = [slice(BANK_TILES * b, BANK_TILES * (b + 1)) for b in range(BANKS)]
            result = results.tile([P, TILES, D], F32)
            squares = work.tile([P, TILES, D], BF16)
            square_sum = stats.tile([P, BANK_TILES], F32)
            moments = stats.tile([P, BANK_TILES, 3], F32)
            rstd2 = stats.tile([P, TILES], F32)
            shift = stats.tile([P, TILES], F32)
            nc.vector.bn_stats(
                out=moments[:].rearrange("p a m -> p (a m)"),
                in_=z_of[g][:, pairs[1], :].rearrange("p a d -> p d a"),
            )
            for j in range(BANK_TILES):
                squares_of_tile(g, j, squares, square_sum)
            root_of_squares(rstd2[:, pairs[0]], square_sum[:])
            nc.scalar.activation(
                out=rstd2[:, pairs[1]],
                in_=moments[:, :, 2],
                func=ACT.Abs_reciprocal_sqrt,
                scale=1.0 / float(D),
                bias=eps_ln[:, 0:1],
            )
            shift_of_sums(shift[:, pairs[0]], z_sum_of[g][:, pairs[0]], rstd2[:, pairs[0]])
            finish_pair(g, 0, [nc.vector, nc.scalar], result, rstd2, shift)
            nc.vector.scalar_tensor_tensor(
                out=shift[:, pairs[1]],
                in0=moments[:, :, 1],
                scalar=-1.0,
                in1=rstd2[:, pairs[1]],
                op0=ALU.mult,
                op1=ALU.mult,
            )
            finish_pair(g, 1, [nc.vector, nc.scalar], result, rstd2, shift)

        def run(stage, g, *more):
            if 0 <= g < GROUPS:
                stage(g, *more)

        def step(s):
            run(second_squares, s - 1)
            run(second_root, s - 1)
            run(second_shift, s - 2)
            run(centre, s)
            run(first_moments, s + 1)
            run(first_moments_scalar, s + 1)
            run(residual, s)
            run(turn, s + 4)
            run(regroup, s + 3, 0)
            run(regroup, s + 3, 1)
            run(first_root, s + 1)
            run(finish, s - 2)
            run(quantise, s + 2)
            run(multiply, s + 2)

        with tc.manual_schedule(engines={mybir.EngineType.PE}):
            turn(0)
            turn(1)
            make_gain()
            quantise_decoder()
            regroup(0, 0)
            regroup(0, 1)
            quantise(0)
            multiply(0)
            turn(2)
            regroup(1, 0)
            regroup(1, 1)
            first_moments(0)
            first_moments_scalar(0)
            first_root(0)
            quantise(1)
            multiply(1)
            turn(3)
            regroup(2, 0)
            regroup(2, 1)
        compute = {
            mybir.EngineType.PE,
            mybir.EngineType.Activation,
            mybir.EngineType.DVE,
            mybir.EngineType.Pool,
        }
        with tc.manual_schedule(engines=compute):
            last = GROUPS - 1
            for s in range(last - 1):
                step(s)

            second_squares(last - 2)
            second_root(last - 2)
            second_shift(last - 3)
            centre(last - 1)
            first_moments(last)
            first_moments_scalar(last)
            first_root(last)
            finish(last - 3)
            second_shift(last - 2)
            residual(last - 1)
            finish_by_pairs(last - 2, [nc.scalar, nc.vector])

            second_squares(last - 1)
            second_root(last - 1)
            centre(last)
            second_shift(last - 1)
            residual(last)
            finish_by_pairs(last - 1, [nc.scalar, nc.scalar])
            second_norm_of_last(last)
